import numpy as np
import ml_dtypes


def mxq(x, axis, fmt="e4m3"):
    dtype, down = {"e4m3": (ml_dtypes.float8_e4m3fn, 7), "e5m2": (ml_dtypes.float8_e5m2, 14)}[fmt]
    v = np.moveaxis(np.asarray(x, np.float32).astype(ml_dtypes.bfloat16).astype(np.float64), axis, -1)
    blocks = v.reshape(v.shape[:-1] + (-1, 32))
    amax = np.abs(blocks).max(-1, keepdims=True)
    byte = np.maximum(np.where(amax > 0, np.frexp(amax)[1] - 1 + 127, 0) - down, 1)
    scale = np.exp2(byte - 127.0)
    codes = (blocks / scale).astype(np.float32).astype(dtype).astype(np.float64)
    return np.moveaxis((codes * scale).reshape(v.shape), -1, axis)


WIDE = False


def mx_kscale(k):
    if not WIDE:
        return np.ones(k)
    levels = np.array([10, -10, 5, -5, 0])
    if k % 512:
        return np.exp2(np.random.permutation(np.resize(levels, k // 32))).repeat(32)
    a = np.empty((k // 512, 16))
    for p in range(k // 512):
        a[p, :8] = np.random.permutation(np.resize(levels, 8))
        for g in range(8):
            far = levels[np.abs(levels - a[p, g]) >= 10]
            a[p, g + 8] = far[np.random.randint(len(far))]
    return np.exp2(a.ravel()).repeat(32)


BF16 = ml_dtypes.bfloat16


def bf(x):
    return np.asarray(x, np.float32).astype(BF16)


def f64(x):
    return np.asarray(x).astype(np.float64)


B, H, L, DM, DK, DV = 2, 2, 512, 512, 512, 1024


def rotate_every_two(x):
    x1 = x[..., ::2]
    x2 = x[..., 1::2]
    return np.stack((-x2, x1), axis=-1).reshape(x.shape)


def xpos_sincos(length, dim):
    angle = 1.0 / (10000.0 ** np.linspace(0.0, 1.0, dim // 2))
    angle = np.repeat(angle, 2)
    idx = f64(np.arange(length))
    angles = idx[:, None] * angle[None, :]
    return np.sin(angles), np.cos(angles)


def draw0():
    s = mx_kscale(DM)
    return {"X": bf(np.random.standard_normal((B, H, L, DM)) * s),
            "W_Q": bf(np.random.standard_normal((DM, DK)) * 3.0 / np.sqrt(DM) / s[:, None]),
            "W_K": bf(np.random.standard_normal((DM, DK)) * 3.0 / np.sqrt(DM) / s[:, None])}


def core(X, W_Q, W_K):
    xq = mxq(f64(X), 3, "e4m3")
    q = xq @ mxq(f64(W_Q), 0, "e4m3")
    k = xq @ mxq(f64(W_K), 0, "e4m3")
    sin, cos = xpos_sincos(L, DK)
    q_rot = q * cos + rotate_every_two(q) * sin
    k_rot = k * cos + rotate_every_two(k) * (-sin)
    return (q_rot, k_rot)


def e4m3fn_bytes(y):
    return np.clip(np.asarray(y, np.float64), -448.0, 448.0).astype(np.float32).astype(ml_dtypes.float8_e4m3fn).view(np.uint8)


def e4m3fn_values(b):
    return np.asarray(b, np.uint8).view(ml_dtypes.float8_e4m3fn).astype(np.float64)


def setup_inputs():
    d = draw0()
    x0 = np.asarray(d['X']).astype(np.float64)
    s = (np.max(np.abs(x0), axis=(0, 1, 2), keepdims=True) / 448.0).astype(np.float32)
    out = {}
    for k, v in d.items():
        if k == 'X':
            out['X_bytes'] = e4m3fn_bytes(x0 / s.astype(np.float64))
            out['X_scale'] = s
        else:
            out[k] = v
    return out


def reference(X_bytes, X_scale, W_Q, W_K):
    return core(e4m3fn_values(X_bytes) * X_scale.astype(np.float64), W_Q, W_K)

@@ -1,0 +1,363 @@
+import math
+from contextlib import ExitStack
+
+import concourse.mybir as mybir
+from concourse.masks import make_identity
+
+FLOPS = 2 * 2 * 2048 * 512 * 512
+
+F32 = mybir.dt.float32
+BF16 = mybir.dt.bfloat16
+I32 = mybir.dt.int32
+U32 = mybir.dt.uint32
+U8 = mybir.dt.uint8
+FP8 = mybir.dt.float8_e4m3fn
+FP8X4 = mybir.dt.float8_e4m3fn_x4
+ALU = mybir.AluOpType
+ACT = mybir.ActivationFunctionType
+
+P = 128
+D = 512
+HALF = 256
+N_LT = 4
+N_BH = 4
+N_ROWS = 16
+N_PAIRS = 8
+TWO_PI = 2.0 * math.pi
+ROOT2 = math.sqrt(2.0)
+RATIO = 10000.0 ** (-1.0 / 255.0)
+PHASES = (-0.125, 0.625, 0.25)
+DIRECT_BIAS = (-0.25 * math.pi, -0.75 * math.pi, 0.5 * math.pi)
+T_HALVES = ((1, 0), (8, 0), (11, 0), (13, 0))
+V_HALVES = ((14, 1), (15, 0), (15, 1))
+G_WEAVES = (0,)
+
+
+def first_direct(a):
+    return min([i for i in range(0, HALF, 8) if (P * a + P - 1) * RATIO**i <= 1.2 * math.pi])
+
+
+def tile_retention_pa_kernel(tc, X_bytes, X_scale, W_Q, W_K, out_0, out_1):
+    nc = tc.nc
+    x_view = X_bytes.rearrange("b h (a p) k -> a p (b h) k", p=P)
+    o_views = (
+        out_0.rearrange("b h (a p) d -> a (b h) p d", p=P),
+        out_1.rearrange("b h (a p) d -> a (b h) p d", p=P),
+    )
+
+    with ExitStack() as ctx:
+        const = ctx.enter_context(tc.tile_pool(name="const", bufs=1))
+        work = ctx.enter_context(tc.tile_pool(name="work", bufs=3))
+        psum = ctx.enter_context(tc.psum_pool(name="psum", bufs=2))
+
+        x_bytes = []
+        for a in range(N_LT):
+            xb = const.tile([P, N_BH, D], U8, name="x_bytes%d" % a)
+            x_bytes.append(xb)
+        nc.sync.dma_start(out=x_bytes[0][:], in_=x_view[0])
+        scale_pt = const.tile([P, 4], F32, name="scale_pt")
+        nc.sync.dma_start(out=scale_pt[:], in_=X_scale.rearrange("a b c (p t) -> p (a b c t)", t=4))
+        w_raw = []
+        for n, w in enumerate((W_Q, W_K)):
+            wr = const.tile([P, 4, D], BF16, name="w_raw%d" % n)
+            nc.sync.dma_start(out=wr[:], in_=w.rearrange("(p j) n -> p j n", j=4))
+            w_raw.append(wr)
+        for a in range(1, N_LT):
+            nc.sync.dma_start(out=x_bytes[a][:], in_=x_view[a])
+
+        ones = const.tile([P, 16], F32, name="ones")
+        nc.vector.memset(ones[:], 1.0)
+        warm = const.tile([P, 1], F32, name="warm")
+        nc.scalar.activation(out=warm[:], in_=ones[:, 0:1], func=ACT.Sin)
+        digits = const.tile([P, 16], F32, name="digits")
+        nc.vector.memset(digits[:], 1.0)
+        l_int = const.tile([P, N_LT], I32, name="l_int")
+        nc.gpsimd.iota(l_int[:], pattern=[[P, N_LT]], base=0, channel_multiplier=1)
+        ident32 = const.tile([P, P], F32, name="ident32")
+        make_identity(nc, ident32[:])
+
+        ctx.enter_context(tc.manual_schedule())
+
+        l_col = const.tile([P, N_LT], F32, name="l_col")
+        nc.vector.tensor_copy(out=l_col[:], in_=l_int[:])
+        for level in range(4):
+            for n in range(4):
+                value = RATIO ** (n * 4**level)
+                if level == 0:
+                    value = value / TWO_PI
+                elif n == 0:
+                    continue
+                c = 4 * level + n
+                nc.vector.tensor_scalar(
+                    out=digits[:, c : c + 1], in0=ones[:, 0:1],
+                    scalar1=value, scalar2=None, op0=ALU.mult,
+                )
+        low = const.tile([P, 16], F32, name="low")
+        high = const.tile([P, 16], F32, name="high")
+        for dst, base in ((low, 0), (high, 8)):
+            nc.vector.tensor_tensor(
+                out=dst[:].rearrange("p (m n) -> p m n", n=4),
+                in0=digits[:, base + 4 : base + 8].unsqueeze(2).to_broadcast([P, 4, 4]),
+                in1=digits[:, base : base + 4].unsqueeze(1).to_broadcast([P, 4, 4]),
+                op=ALU.mult,
+            )
+        turns = const.tile([P, HALF], F32, name="turns")
+        nc.vector.tensor_tensor(
+            out=turns[:].rearrange("p (m n) -> p m n", n=16),
+            in0=high[:].unsqueeze(2).to_broadcast([P, 16, 16]),
+            in1=low[:].unsqueeze(1).to_broadcast([P, 16, 16]),
+            op=ALU.mult,
+        )
+
+        omega = const.tile([P, HALF], F32, name="omega")
+        nc.vector.tensor_scalar(out=omega[:], in0=turns[:], scalar1=TWO_PI, scalar2=None, op0=ALU.mult)
+        l_neg = const.tile([P, N_LT], F32, name="l_neg")
+        nc.vector.tensor_scalar(out=l_neg[:], in0=l_col[:], scalar1=-1.0, scalar2=None, op0=ALU.mult)
+
+        whole = {}
+        frac = {}
+        tables = {}
+
+        def table_whole(a):
+            cut = first_direct(a)
+            wh = const.tile([P, 3, cut], U32, name="whole%d" % a)
+            for j, phi in enumerate(PHASES):
+                nc.scalar.activation(
+                    out=wh[:, j, :], in_=turns[:, 0:cut], func=ACT.Copy,
+                    scale=l_col[:, a : a + 1], bias=phi,
+                )
+            whole[a] = wh
+
+        def table_frac(a):
+            cut = first_direct(a)
+            fr = const.tile([P, 3, cut], F32, name="frac%d" % a)
+            nc.vector.scalar_tensor_tensor(
+                out=fr[:], in0=turns[:, 0:cut].unsqueeze(1).to_broadcast([P, 3, cut]),
+                scalar=l_col[:, a : a + 1], in1=whole[a][:].bitcast(I32),
+                op0=ALU.mult, op1=ALU.subtract,
+            )
+            frac[a] = fr
+
+        def table_sin(a):
+            tp = const.tile([P, 3, HALF], F32, name="table%d" % a)
+            tables[a] = tp
+            cut = first_direct(a)
+            for j, phi in enumerate(PHASES):
+                l_signed = l_neg if j == 2 else l_col
+                pieces = (
+                    (0, cut, frac[a][:, j, :], TWO_PI, TWO_PI * phi),
+                    (cut, HALF, omega[:, cut:HALF], l_signed[:, a : a + 1], DIRECT_BIAS[j]),
+                )
+                for lo, hi, src, scale, bias in pieces:
+                    nc.scalar.activation(out=tp[:, j, lo:hi], in_=src, func=ACT.Sin, scale=scale, bias=bias)
+
+        w_grouped = {}
+        w_codes = {}
+        w_scales = {}
+
+        def weight_copy(n):
+            wg = const.tile([P, 4 * D], BF16, name="w_grouped%d" % n, align_bytes=64)
+            for h in range(2):
+                nc.vector.tensor_copy(
+                    out=wg[:, h * 1024 : (h + 1) * 1024].rearrange("p (i t) -> p i t", t=4),
+                    in_=w_raw[n][:].rearrange("p t (i e) -> p e i t", e=2)[:, 1 - h],
+                )
+            w_grouped[n] = wg
+
+        def weight_quant(n):
+            wc = const.tile([P, D], U32, name="w_codes%d" % n, align_bytes=64)
+            ws = const.tile([P, D], U8, name="w_scales%d" % n, align_bytes=64)
+            nc.vector.quantize_mx(out=wc[:].bitcast(FP8X4), scales=ws[:], in_=w_grouped[n][:])
+            w_codes[n] = wc
+            w_scales[n] = ws
+
+        wide = {}
+        turned = {}
+        grouped = {}
+        x_codes = {}
+
+        def x_cast(j):
+            a, first = j // 2, 2 * (j % 2)
+            wd = work.tile([P, 2 * D], BF16, name="wide", tag="wide")
+            nc.scalar.copy(
+                out=wd[:],
+                in_=x_bytes[a][:, first : first + 2, :].rearrange("p b k -> p (b k)").bitcast(FP8),
+            )
+            wide[j] = wd
+
+        def x_turn(j):
+            xt = psum.tile([P, 2, 2, P], F32, name="xt", tag="xt", bufs=1)
+            words = wide[j][:].bitcast(F32)
+            for s in range(2):
+                for u in range(2):
+                    nc.tensor.transpose(xt[:, u, s, :], words[:, s * HALF + u : (s + 1) * HALF : 2], ident32[:])
+            turned[j] = xt
+
+        def x_scale(j):
+            planes = work.tile([P, 4, 2 * P], BF16, name="planes", tag="planes", bufs=2)
+            for t in range(4):
+                nc.scalar.activation(
+                    out=planes[:, t, :],
+                    in_=turned[j][:, t // 2].rearrange("p s r -> p (s r)").bitcast(BF16)
+                    .rearrange("p (c e) -> p c e", e=2)[:, :, t % 2],
+                    func=ACT.Copy, scale=scale_pt[:, t : t + 1],
+                )
+            turned[j] = planes
+
+        def x_weave(j):
+            gr = work.tile([P, 1024], BF16, name="grouped", tag="grouped", align_bytes=64)
+            if j in G_WEAVES:
+                nc.gpsimd.tensor_scalar(
+                    out=gr[:].rearrange("p (c t) -> p c t", t=4),
+                    in0=turned[j][:].rearrange("p t c -> p c t"),
+                    scalar1=1.0, scalar2=0.0, op0=ALU.mult, op1=ALU.add,
+                )
+            else:
+                nc.scalar.copy(
+                    out=gr[:].rearrange("p (c t) -> p c t", t=4),
+                    in_=turned[j][:].rearrange("p t c -> p c t"),
+                )
+            grouped[j] = gr
+
+        def x_quant(j):
+            xc = work.tile([P, HALF], U32, name="xc", tag="xc", align_bytes=64)
+            xsc = work.tile([P, HALF], U8, name="xsc", tag="xsc", align_bytes=64)
+            nc.vector.quantize_mx(out=xc[:].bitcast(FP8X4), scales=xsc[:], in_=grouped[j][:])
+            x_codes[j] = (xc, xsc)
+
+        banks = {}
+        parts = {}
+        results = {}
+
+        def mx(r):
+            xc, xsc = x_codes[r // 2]
+            rows = slice((r % 2) * P, (r % 2 + 1) * P)
+            lhs = xc[:, rows].bitcast(FP8X4)
+            lhs_s = xsc[:, rows]
+            got = []
+            for n in range(2):
+                acc = psum.tile([P, D], F32, name="acc%d" % n, tag="acc%d" % n)
+                nc.tensor.matmul_mx(
+                    out=acc[:], lhsT=lhs, lhsT_scale=lhs_s,
+                    rhs=w_codes[n][:].bitcast(FP8X4), rhs_scale=w_scales[n][:],
+                    start=True, stop=True,
+                )
+                got.append(acc)
+            sums = psum.tile([P, D], F32, name="sums", tag="sums")
+            for n in range(2):
+                for h in range(2):
+                    cols = slice(h * HALF, (h + 1) * HALF)
+                    nc.tensor.matmul_mx(
+                        out=sums[:, n * HALF : (n + 1) * HALF], lhsT=lhs, lhsT_scale=lhs_s,
+                        rhs=w_codes[n][:, cols].bitcast(FP8X4), rhs_scale=w_scales[n][:, cols],
+                        start=(h == 0), stop=(h == 1),
+                    )
+            got.append(sums)
+            banks[r] = got
+
+        def mul(r):
+            tp = tables[r // 4]
+            cross = work.tile([P, 2 * D], F32, name="cross", tag="cross", bufs=6)
+            pair = tp[:, 0:2, :].rearrange("p e i -> p i e")
+            for n in range(2):
+                nc.vector.scalar_tensor_tensor(
+                    out=cross[:, n * D : (n + 1) * D].rearrange("p (i e) -> p i e", e=2),
+                    in0=banks[r][n][:].rearrange("p (e i) -> p i e", e=2),
+                    scalar=ROOT2,
+                    in1=pair if n == 1 else pair[:, :, ::-1],
+                    op0=ALU.mult, op1=ALU.mult,
+                )
+            common = work.tile([P, D], F32, name="common", tag="common", bufs=6)
+            nc.vector.tensor_tensor(
+                out=common[:].rearrange("p (n i) -> p n i", n=2),
+                in0=banks[r][2][:].rearrange("p (n i) -> p n i", n=2),
+                in1=tp[:, 2:3, :].to_broadcast([P, 2, HALF]),
+                op=ALU.mult,
+            )
+            parts[r] = (cross, common)
+            res = work.tile([P, 2 * D], F32, name="res", tag="res", bufs=7)
+            results[r] = res
+
+        def store(r, n, queue):
+            queue.dma_start(out=o_views[n][r // 4, r % 4], in_=results[r][:, n * D : (n + 1) * D])
+
+        def add_on(engine, r, first, count):
+            cross, common = parts[r]
+            nc_cols = slice(first * D, (first + count) * D)
+            engine.tensor_tensor(
+                out=results[r][:, nc_cols].rearrange("p (m e) -> p m e", e=2),
+                in0=common[:, first * HALF : (first + count) * HALF].unsqueeze(2).to_broadcast([P, count * HALF, 2]),
+                in1=cross[:, nc_cols].rearrange("p (m e) -> p m e", e=2),
+                op=ALU.add,
+            )
+
+        added = {}
+
+        def add_tensor(r):
+            cross, common = parts[r]
+            total = psum.tile([P, D], F32, name="total", tag="total", bufs=1)
+            nc.tensor.matmul(out=total[:], lhsT=ident32[:], rhs=cross[:, 0:D], start=True, stop=False)
+            nc.tensor.matmul(
+                out=total[:].rearrange("p (m e) -> p m e", e=2), lhsT=ident32[:],
+                rhs=common[:, 0:HALF].unsqueeze(2).to_broadcast([P, HALF, 2]),
+                start=False, stop=True,
+            )
+            added[r] = total
+
+        def add_tensor_out(r):
+            nc.scalar.copy(out=results[r][:, 0:D], in_=added[r][:])
+            store(r, 0, nc.scalar)
+
+        table_whole(0)
+        table_frac(0)
+        x_cast(0)
+        x_turn(0)
+        x_cast(1)
+        x_scale(0)
+        x_weave(0)
+        weight_copy(0)
+        weight_quant(0)
+        weight_copy(1)
+        x_quant(0)
+        weight_quant(1)
+        table_sin(0)
+        x_turn(1)
+        x_scale(1)
+        x_weave(1)
+        x_cast(2)
+        table_whole(1)
+        mx(0)
+        for r in range(N_ROWS):
+            j = r // 2
+            if r % 2 == 0:
+                if j + 2 < N_PAIRS:
+                    x_turn(j + 2)
+                if j + 3 < N_PAIRS:
+                    x_cast(j + 3)
+            if r + 1 < N_ROWS:
+                mx(r + 1)
+            if (r - 1, 0) in T_HALVES:
+                add_tensor(r - 1)
+            mul(r)
+            if r % 2 == 0:
+                if j + 1 < N_PAIRS:
+                    x_quant(j + 1)
+                if j % 2 == 0 and j // 2 + 1 < N_LT:
+                    table_frac(j // 2 + 1)
+            for n in range(2):
+                if (r, n) in V_HALVES:
+                    add_on(nc.vector, r, n, 1)
+                    store(r, n, nc.scalar)
+                elif (r, n) not in T_HALVES:
+                    add_on(nc.gpsimd, r, n, 1)
+                    store(r, n, nc.sync)
+            if r % 2 == 0:
+                if j + 2 < N_PAIRS:
+                    x_scale(j + 2)
+                    x_weave(j + 2)
+            elif j % 2 == 0 and j // 2 + 1 < N_LT:
+                table_sin(j // 2 + 1)
+            elif j % 2 == 1 and j // 2 + 2 < N_LT:
+                table_whole(j // 2 + 2)
+            if (r - 1, 0) in T_HALVES:
+                add_tensor_out(r - 1)

@@ -28,9 +28,10 @@ ROOT2 = math.sqrt(2.0)
 RATIO = 10000.0 ** (-1.0 / 255.0)
 PHASES = (-0.125, 0.625, 0.25)
 DIRECT_BIAS = (-0.25 * math.pi, -0.75 * math.pi, 0.5 * math.pi)
-T_HALVES = ((1, 0), (8, 0), (11, 0), (13, 0))
 V_HALVES = ((14, 1), (15, 0), (15, 1))
 G_WEAVES = (0,)
+PAIRS = ((0, 0), (0, 1), (1, 0), (1, 1), (2, 0), (3, 0), (2, 1), (3, 1))
+TURNED = 2
 
 
 def first_direct(a):
@@ -73,6 +74,8 @@ def tile_retention_pa_kernel(tc, X_bytes, X_scale, W_Q, W_K, out_0, out_1):
         nc.vector.memset(digits[:], 1.0)
         l_int = const.tile([P, N_LT], I32, name="l_int")
         nc.gpsimd.iota(l_int[:], pattern=[[P, N_LT]], base=0, channel_multiplier=1)
+        row_int = const.tile([P, P], I32, name="row_int")
+        nc.gpsimd.iota(row_int[:], pattern=[[1, P]], base=TURNED * P, channel_multiplier=0)
         ident32 = const.tile([P, P], F32, name="ident32")
         make_identity(nc, ident32[:])
 
@@ -151,6 +154,61 @@ def tile_retention_pa_kernel(tc, X_bytes, X_scale, W_Q, W_K, out_0, out_1):
                 for lo, hi, src, scale, bias in pieces:
                     nc.scalar.activation(out=tp[:, j, lo:hi], in_=src, func=ACT.Sin, scale=scale, bias=bias)
 
+        turned_consts = {}
+
+        def turned_prepare_tensor():
+            vt = psum.tile([P, 2, P], F32, name="vt", tag="aux")
+            for tau in range(2):
+                nc.tensor.transpose(vt[:, tau, :], turns[:, tau * P : (tau + 1) * P], ident32[:])
+            turned_consts["vt"] = vt
+
+        def turned_prepare_vector():
+            v_col = const.tile([P, 2], F32, name="v_col")
+            nc.vector.tensor_copy(out=v_col[:], in_=turned_consts["vt"][:, :, 0])
+            w_col = const.tile([P, 2], F32, name="w_col")
+            nc.vector.tensor_scalar(out=w_col[:], in0=v_col[:], scalar1=TWO_PI, scalar2=None, op0=ALU.mult)
+            w_neg = const.tile([P, 2], F32, name="w_neg")
+            nc.vector.tensor_scalar(out=w_neg[:], in0=v_col[:], scalar1=-TWO_PI, scalar2=None, op0=ALU.mult)
+            l_row = const.tile([P, P], F32, name="l_row")
+            nc.vector.tensor_copy(out=l_row[:], in_=row_int[:])
+            turned_consts["v_col"] = v_col
+            turned_consts["w_col"] = w_col
+            turned_consts["w_neg"] = w_neg
+            turned_consts["l_row"] = l_row
+
+        def turned_whole():
+            wh = const.tile([P, 3, P], U32, name="whole_t")
+            for j, phi in enumerate(PHASES):
+                nc.scalar.activation(
+                    out=wh[:, j, :], in_=turned_consts["l_row"][:], func=ACT.Copy,
+                    scale=turned_consts["v_col"][:, 0:1], bias=phi,
+                )
+            turned_consts["whole"] = wh
+
+        def turned_frac():
+            fr = const.tile([P, 3, P], F32, name="frac_t")
+            nc.vector.scalar_tensor_tensor(
+                out=fr[:], in0=turned_consts["l_row"][:].unsqueeze(1).to_broadcast([P, 3, P]),
+                scalar=turned_consts["v_col"][:, 0:1], in1=turned_consts["whole"][:].bitcast(I32),
+                op0=ALU.mult, op1=ALU.subtract,
+            )
+            turned_consts["frac"] = fr
+
+        def turned_sin():
+            assert first_direct(TURNED) <= P
+            tp = const.tile([P, 3, 2, P], F32, name="table_t")
+            for j, phi in enumerate(PHASES):
+                nc.scalar.activation(
+                    out=tp[:, j, 0, :], in_=turned_consts["frac"][:, j, :], func=ACT.Sin,
+                    scale=TWO_PI, bias=TWO_PI * phi,
+                )
+                w_signed = turned_consts["w_neg"] if j == 2 else turned_consts["w_col"]
+                nc.scalar.activation(
+                    out=tp[:, j, 1, :], in_=turned_consts["l_row"][:], func=ACT.Sin,
+                    scale=w_signed[:, 1:2], bias=DIRECT_BIAS[j],
+                )
+            turned_consts["table"] = tp
+
         w_grouped = {}
         w_codes = {}
         w_scales = {}
@@ -177,7 +235,7 @@ def tile_retention_pa_kernel(tc, X_bytes, X_scale, W_Q, W_K, out_0, out_1):
         x_codes = {}
 
         def x_cast(j):
-            a, first = j // 2, 2 * (j % 2)
+            a, first = PAIRS[j][0], 2 * PAIRS[j][1]
             wd = work.tile([P, 2 * D], BF16, name="wide", tag="wide")
             nc.scalar.copy(
                 out=wd[:],
@@ -186,7 +244,7 @@ def tile_retention_pa_kernel(tc, X_bytes, X_scale, W_Q, W_K, out_0, out_1):
             wide[j] = wd
 
         def x_turn(j):
-            xt = psum.tile([P, 2, 2, P], F32, name="xt", tag="xt", bufs=1)
+            xt = psum.tile([P, 2, 2, P], F32, name="xt", tag="aux")
             words = wide[j][:].bitcast(F32)
             for s in range(2):
                 for u in range(2):
@@ -256,7 +314,7 @@ def tile_retention_pa_kernel(tc, X_bytes, X_scale, W_Q, W_K, out_0, out_1):
             banks[r] = got
 
         def mul(r):
-            tp = tables[r // 4]
+            tp = tables[PAIRS[r // 2][0]]
             cross = work.tile([P, 2 * D], F32, name="cross", tag="cross", bufs=6)
             pair = tp[:, 0:2, :].rearrange("p e i -> p i e")
             for n in range(2):
@@ -279,7 +337,8 @@ def tile_retention_pa_kernel(tc, X_bytes, X_scale, W_Q, W_K, out_0, out_1):
             results[r] = res
 
         def store(r, n, queue):
-            queue.dma_start(out=o_views[n][r // 4, r % 4], in_=results[r][:, n * D : (n + 1) * D])
+            a, half = PAIRS[r // 2]
+            queue.dma_start(out=o_views[n][a, 2 * half + r % 2], in_=results[r][:, n * D : (n + 1) * D])
 
         def add_on(engine, r, first, count):
             cross, common = parts[r]
@@ -291,25 +350,89 @@ def tile_retention_pa_kernel(tc, X_bytes, X_scale, W_Q, W_K, out_0, out_1):
                 op=ALU.add,
             )
 
+        def mx_turned(r):
+            xc, xsc = x_codes[r // 2]
+            rows = slice((r % 2) * P, (r % 2 + 1) * P)
+            rhs = xc[:, rows].bitcast(FP8X4)
+            rhs_s = xsc[:, rows]
+            got = []
+            for n in range(2):
+                acc = psum.tile([P, D], F32, name="acc%d" % n, tag="acc%d" % n)
+                for blk in range(4):
+                    cols = slice(blk * P, (blk + 1) * P)
+                    nc.tensor.matmul_mx(
+                        out=acc[:, cols], lhsT=w_codes[n][:, cols].bitcast(FP8X4), lhsT_scale=w_scales[n][:, cols],
+                        rhs=rhs, rhs_scale=rhs_s, start=True, stop=True,
+                    )
+                got.append(acc)
+            sums = psum.tile([P, D], F32, name="sums", tag="sums")
+            for n in range(2):
+                for tau in range(2):
+                    for h in range(2):
+                        cols = slice((2 * h + tau) * P, (2 * h + tau + 1) * P)
+                        nc.tensor.matmul_mx(
+                            out=sums[:, (2 * n + tau) * P : (2 * n + tau + 1) * P],
+                            lhsT=w_codes[n][:, cols].bitcast(FP8X4), lhsT_scale=w_scales[n][:, cols],
+                            rhs=rhs, rhs_scale=rhs_s, start=(h == 0), stop=(h == 1),
+                        )
+            got.append(sums)
+            banks[r] = got
+
+        def mul_turned(r):
+            tp = turned_consts["table"]
+            cross = work.tile([P, 2 * D], F32, name="cross", tag="cross", bufs=6)
+            pair = tp[:, 0:2].rearrange("p e t l -> p e (t l)")
+            for n in range(2):
+                nc.vector.scalar_tensor_tensor(
+                    out=cross[:, n * D : (n + 1) * D].rearrange("p (e m) -> p e m", e=2),
+                    in0=banks[r][n][:].rearrange("p (e m) -> p e m", e=2),
+                    scalar=ROOT2,
+                    in1=pair if n == 1 else pair[:, ::-1, :],
+                    op0=ALU.mult, op1=ALU.mult,
+                )
+            common = work.tile([P, D], F32, name="common", tag="common", bufs=6)
+            nc.vector.tensor_tensor(
+                out=common[:].rearrange("p (n m) -> p n m", n=2),
+                in0=banks[r][2][:].rearrange("p (n m) -> p n m", n=2),
+                in1=tp[:, 2:3].rearrange("p e t l -> p e (t l)").to_broadcast([P, 2, HALF]),
+                op=ALU.mult,
+            )
+            parts[r] = (cross, common)
+            res = work.tile([P, 2 * D], F32, name="res", tag="res", bufs=7)
+            results[r] = res
+
         added = {}
 
-        def add_tensor(r):
+        def turn_add(r, n):
             cross, common = parts[r]
-            total = psum.tile([P, D], F32, name="total", tag="total", bufs=1)
-            nc.tensor.matmul(out=total[:], lhsT=ident32[:], rhs=cross[:, 0:D], start=True, stop=False)
-            nc.tensor.matmul(
-                out=total[:].rearrange("p (m e) -> p m e", e=2), lhsT=ident32[:],
-                rhs=common[:, 0:HALF].unsqueeze(2).to_broadcast([P, HALF, 2]),
-                start=False, stop=True,
+            total = psum.tile([P, D], F32, name="total", tag="aux")
+            for e in range(2):
+                for tau in range(2):
+                    region = total[:, (2 * e + tau) * P : (2 * e + tau + 1) * P]
+                    nc.tensor.matmul(
+                        out=region, lhsT=common[:, (2 * n + tau) * P : (2 * n + tau + 1) * P], rhs=ident32[:],
+                        is_transpose=True, start=True, stop=False,
+                    )
+                    nc.tensor.matmul(
+                        out=region, lhsT=cross[:, n * D + (2 * e + tau) * P : n * D + (2 * e + tau + 1) * P],
+                        rhs=ident32[:], is_transpose=True, start=False, stop=True,
+                    )
+            added[(r, n)] = total
+
+        def turn_add_out(r, n):
+            nc.scalar.copy(
+                out=results[r][:, n * D : (n + 1) * D].rearrange("p (m e) -> p m e", e=2),
+                in_=added[(r, n)][:].rearrange("p (e m) -> p m e", e=2),
             )
-            added[r] = total
+            store(r, n, nc.scalar)
 
-        def add_tensor_out(r):
-            nc.scalar.copy(out=results[r][:, 0:D], in_=added[r][:])
-            store(r, 0, nc.scalar)
+        def is_turned(r):
+            return PAIRS[r // 2][0] == TURNED
 
+        turned_prepare_tensor()
         table_whole(0)
         table_frac(0)
+        turned_prepare_vector()
         x_cast(0)
         x_turn(0)
         x_cast(1)
@@ -327,6 +450,12 @@ def tile_retention_pa_kernel(tc, X_bytes, X_scale, W_Q, W_K, out_0, out_1):
         x_cast(2)
         table_whole(1)
         mx(0)
+        fractions = {0: lambda: table_frac(1), 4: turned_frac, 6: lambda: table_frac(3)}
+        scalar_tables = {
+            1: (lambda: table_sin(1),), 3: (turned_whole,), 5: (turned_sin, lambda: table_whole(3)),
+            7: (lambda: table_sin(3),),
+        }
+        waiting = []
         for r in range(N_ROWS):
             j = r // 2
             if r % 2 == 0:
@@ -335,29 +464,39 @@ def tile_retention_pa_kernel(tc, X_bytes, X_scale, W_Q, W_K, out_0, out_1):
                 if j + 3 < N_PAIRS:
                     x_cast(j + 3)
             if r + 1 < N_ROWS:
-                mx(r + 1)
-            if (r - 1, 0) in T_HALVES:
-                add_tensor(r - 1)
-            mul(r)
+                if is_turned(r + 1):
+                    mx_turned(r + 1)
+                else:
+                    mx(r + 1)
+            now = waiting[0:1] if r + 1 < N_ROWS else waiting[:]
+            for unit in now:
+                waiting.remove(unit)
+                turn_add(unit[0], unit[1])
+            if is_turned(r):
+                mul_turned(r)
+                waiting.extend([(r, 0), (r, 1)])
+            else:
+                mul(r)
             if r % 2 == 0:
                 if j + 1 < N_PAIRS:
                     x_quant(j + 1)
-                if j % 2 == 0 and j // 2 + 1 < N_LT:
-                    table_frac(j // 2 + 1)
-            for n in range(2):
-                if (r, n) in V_HALVES:
-                    add_on(nc.vector, r, n, 1)
-                    store(r, n, nc.scalar)
-                elif (r, n) not in T_HALVES:
-                    add_on(nc.gpsimd, r, n, 1)
-                    store(r, n, nc.sync)
+            if r in fractions:
+                fractions[r]()
+            by_vector = [n for n in range(2) if (r, n) in V_HALVES]
+            if not is_turned(r):
+                for n in range(2):
+                    if n in by_vector:
+                        add_on(nc.vector, r, n, 1)
+                    else:
+                        add_on(nc.gpsimd, r, n, 1)
+                        store(r, n, nc.sync)
             if r % 2 == 0:
                 if j + 2 < N_PAIRS:
                     x_scale(j + 2)
                     x_weave(j + 2)
-            elif j % 2 == 0 and j // 2 + 1 < N_LT:
-                table_sin(j // 2 + 1)
-            elif j % 2 == 1 and j // 2 + 2 < N_LT:
-                table_whole(j // 2 + 2)
-            if (r - 1, 0) in T_HALVES:
-                add_tensor_out(r - 1)
+            for step in scalar_tables.get(r, ()):
+                step()
+            for unit in now:
+                turn_add_out(unit[0], unit[1])
+            for n in by_vector:
+                store(r, n, nc.scalar)

@@ -28,7 +28,7 @@ ROOT2 = math.sqrt(2.0)
 RATIO = 10000.0 ** (-1.0 / 255.0)
 PHASES = (-0.125, 0.625, 0.25)
 DIRECT_BIAS = (-0.25 * math.pi, -0.75 * math.pi, 0.5 * math.pi)
-V_HALVES = ((14, 1), (15, 0), (15, 1))
+V_HALVES = ((15, 1),)
 G_WEAVES = (0,)
 PAIRS = ((0, 0), (0, 1), (1, 0), (1, 1), (2, 0), (3, 0), (2, 1), (3, 1))
 TURNED = 2
@@ -316,22 +316,33 @@ def tile_retention_pa_kernel(tc, X_bytes, X_scale, W_Q, W_K, out_0, out_1):
         def mul(r):
             tp = tables[PAIRS[r // 2][0]]
             cross = work.tile([P, 2 * D], F32, name="cross", tag="cross", bufs=6)
-            pair = tp[:, 0:2, :].rearrange("p e i -> p i e")
-            for n in range(2):
-                nc.vector.scalar_tensor_tensor(
-                    out=cross[:, n * D : (n + 1) * D].rearrange("p (i e) -> p i e", e=2),
-                    in0=banks[r][n][:].rearrange("p (e i) -> p i e", e=2),
-                    scalar=ROOT2,
-                    in1=pair if n == 1 else pair[:, :, ::-1],
-                    op0=ALU.mult, op1=ALU.mult,
-                )
             common = work.tile([P, D], F32, name="common", tag="common", bufs=6)
-            nc.vector.tensor_tensor(
-                out=common[:].rearrange("p (n i) -> p n i", n=2),
-                in0=banks[r][2][:].rearrange("p (n i) -> p n i", n=2),
-                in1=tp[:, 2:3, :].to_broadcast([P, 2, HALF]),
-                op=ALU.mult,
-            )
+            pair = tp[:, 0:2, :].rearrange("p e i -> p i e")
+
+            def side_terms():
+                for n in range(2):
+                    nc.vector.scalar_tensor_tensor(
+                        out=cross[:, n * D : (n + 1) * D].rearrange("p (i e) -> p i e", e=2),
+                        in0=banks[r][n][:].rearrange("p (e i) -> p i e", e=2),
+                        scalar=ROOT2,
+                        in1=pair if n == 1 else pair[:, :, ::-1],
+                        op0=ALU.mult, op1=ALU.mult,
+                    )
+
+            def shared_term():
+                nc.vector.tensor_tensor(
+                    out=common[:].rearrange("p (n i) -> p n i", n=2),
+                    in0=banks[r][2][:].rearrange("p (n i) -> p n i", n=2),
+                    in1=tp[:, 2:3, :].to_broadcast([P, 2, HALF]),
+                    op=ALU.mult,
+                )
+
+            if r == N_ROWS - 1:
+                shared_term()
+                side_terms()
+            else:
+                side_terms()
+                shared_term()
             parts[r] = (cross, common)
             res = work.tile([P, 2 * D], F32, name="res", tag="res", bufs=7)
             results[r] = res

@@ -272,8 +272,8 @@ def tile_retention_pa_kernel(tc, X_bytes, X_scale, W_Q, W_K, out_0, out_1):
                 )
             else:
                 nc.scalar.copy(
-                    out=gr[:].rearrange("p (c t) -> p c t", t=4),
-                    in_=turned[j][:].rearrange("p t c -> p c t"),
+                    out=gr[:].rearrange("p (c i t) -> p c t i", i=4, t=4),
+                    in_=turned[j][:].rearrange("p t (c i) -> p c t i", i=4),
                 )
             grouped[j] = gr
 

@@ -265,10 +265,9 @@ def tile_retention_pa_kernel(tc, X_bytes, X_scale, W_Q, W_K, out_0, out_1):
         def x_weave(j):
             gr = work.tile([P, 1024], BF16, name="grouped", tag="grouped", align_bytes=64)
             if j in G_WEAVES:
-                nc.gpsimd.tensor_scalar(
+                nc.vector.tensor_copy(
                     out=gr[:].rearrange("p (c t) -> p c t", t=4),
-                    in0=turned[j][:].rearrange("p t c -> p c t"),
-                    scalar1=1.0, scalar2=0.0, op0=ALU.mult, op1=ALU.add,
+                    in_=turned[j][:].rearrange("p t c -> p c t"),
                 )
             else:
                 nc.scalar.copy(
@@ -448,9 +447,9 @@ def tile_retention_pa_kernel(tc, X_bytes, X_scale, W_Q, W_K, out_0, out_1):
         x_turn(0)
         x_cast(1)
         x_scale(0)
-        x_weave(0)
         weight_copy(0)
         weight_quant(0)
+        x_weave(0)
         weight_copy(1)
         x_quant(0)
         weight_quant(1)

@@ -28,9 +28,9 @@ ROOT2 = math.sqrt(2.0)
 RATIO = 10000.0 ** (-1.0 / 255.0)
 PHASES = (-0.125, 0.625, 0.25)
 DIRECT_BIAS = (-0.25 * math.pi, -0.75 * math.pi, 0.5 * math.pi)
-V_HALVES = ((15, 1),)
+V_HALVES = ()
 G_WEAVES = (0,)
-PAIRS = ((0, 0), (0, 1), (1, 0), (1, 1), (2, 0), (3, 0), (2, 1), (3, 1))
+PAIRS = ((0, 0), (0, 1), (1, 0), (1, 1), (2, 0), (3, 0), (3, 1), (2, 1))
 TURNED = 2
 
 
@@ -365,16 +365,6 @@ def tile_retention_pa_kernel(tc, X_bytes, X_scale, W_Q, W_K, out_0, out_1):
             rows = slice((r % 2) * P, (r % 2 + 1) * P)
             rhs = xc[:, rows].bitcast(FP8X4)
             rhs_s = xsc[:, rows]
-            got = []
-            for n in range(2):
-                acc = psum.tile([P, D], F32, name="acc%d" % n, tag="acc%d" % n)
-                for blk in range(4):
-                    cols = slice(blk * P, (blk + 1) * P)
-                    nc.tensor.matmul_mx(
-                        out=acc[:, cols], lhsT=w_codes[n][:, cols].bitcast(FP8X4), lhsT_scale=w_scales[n][:, cols],
-                        rhs=rhs, rhs_scale=rhs_s, start=True, stop=True,
-                    )
-                got.append(acc)
             sums = psum.tile([P, D], F32, name="sums", tag="sums")
             for n in range(2):
                 for tau in range(2):
@@ -385,12 +375,29 @@ def tile_retention_pa_kernel(tc, X_bytes, X_scale, W_Q, W_K, out_0, out_1):
                             lhsT=w_codes[n][:, cols].bitcast(FP8X4), lhsT_scale=w_scales[n][:, cols],
                             rhs=rhs, rhs_scale=rhs_s, start=(h == 0), stop=(h == 1),
                         )
+            got = []
+            for n in range(2):
+                acc = psum.tile([P, D], F32, name="acc%d" % n, tag="acc%d" % n)
+                for blk in range(4):
+                    cols = slice(blk * P, (blk + 1) * P)
+                    nc.tensor.matmul_mx(
+                        out=acc[:, cols], lhsT=w_codes[n][:, cols].bitcast(FP8X4), lhsT_scale=w_scales[n][:, cols],
+                        rhs=rhs, rhs_scale=rhs_s, start=True, stop=True,
+                    )
+                got.append(acc)
             got.append(sums)
             banks[r] = got
 
         def mul_turned(r):
             tp = turned_consts["table"]
             cross = work.tile([P, 2 * D], F32, name="cross", tag="cross", bufs=6)
+            common = work.tile([P, D], F32, name="common", tag="common", bufs=6)
+            nc.vector.tensor_tensor(
+                out=common[:].rearrange("p (n m) -> p n m", n=2),
+                in0=banks[r][2][:].rearrange("p (n m) -> p n m", n=2),
+                in1=tp[:, 2:3].rearrange("p e t l -> p e (t l)").to_broadcast([P, 2, HALF]),
+                op=ALU.mult,
+            )
             pair = tp[:, 0:2].rearrange("p e t l -> p e (t l)")
             for n in range(2):
                 nc.vector.scalar_tensor_tensor(
@@ -400,13 +407,6 @@ def tile_retention_pa_kernel(tc, X_bytes, X_scale, W_Q, W_K, out_0, out_1):
                     in1=pair if n == 1 else pair[:, ::-1, :],
                     op0=ALU.mult, op1=ALU.mult,
                 )
-            common = work.tile([P, D], F32, name="common", tag="common", bufs=6)
-            nc.vector.tensor_tensor(
-                out=common[:].rearrange("p (n m) -> p n m", n=2),
-                in0=banks[r][2][:].rearrange("p (n m) -> p n m", n=2),
-                in1=tp[:, 2:3].rearrange("p e t l -> p e (t l)").to_broadcast([P, 2, HALF]),
-                op=ALU.mult,
-            )
             parts[r] = (cross, common)
             res = work.tile([P, 2 * D], F32, name="res", tag="res", bufs=7)
             results[r] = res
@@ -478,7 +478,7 @@ def tile_retention_pa_kernel(tc, X_bytes, X_scale, W_Q, W_K, out_0, out_1):
                     mx_turned(r + 1)
                 else:
                     mx(r + 1)
-            now = waiting[0:1] if r + 1 < N_ROWS else waiting[:]
+            now = waiting[0:1]
             for unit in now:
                 waiting.remove(unit)
                 turn_add(unit[0], unit[1])
@@ -487,6 +487,11 @@ def tile_retention_pa_kernel(tc, X_bytes, X_scale, W_Q, W_K, out_0, out_1):
                 waiting.extend([(r, 0), (r, 1)])
             else:
                 mul(r)
+            if r >= N_ROWS - 2:
+                for unit in waiting:
+                    turn_add(unit[0], unit[1])
+                now = now + waiting
+                waiting = []
             if r % 2 == 0:
                 if j + 1 < N_PAIRS:
                     x_quant(j + 1)

@@ -498,7 +498,11 @@ def tile_retention_pa_kernel(tc, X_bytes, X_scale, W_Q, W_K, out_0, out_1):
             if r in fractions:
                 fractions[r]()
             by_vector = [n for n in range(2) if (r, n) in V_HALVES]
-            if not is_turned(r):
+            if not is_turned(r) and PAIRS[j][0] == 3:
+                add_on(nc.gpsimd, r, 0, 2)
+                for n in range(2):
+                    store(r, n, nc.sync)
+            elif not is_turned(r):
                 for n in range(2):
                     if n in by_vector:
                         add_on(nc.vector, r, n, 1)

@@ -66,56 +66,38 @@ def tile_retention_pa_kernel(tc, X_bytes, X_scale, W_Q, W_K, out_0, out_1):
         for a in range(1, N_LT):
             nc.sync.dma_start(out=x_bytes[a][:], in_=x_view[a])
 
-        ones = const.tile([P, 16], F32, name="ones")
+        ones = const.tile([P, 1], F32, name="ones")
         nc.vector.memset(ones[:], 1.0)
         warm = const.tile([P, 1], F32, name="warm")
-        nc.scalar.activation(out=warm[:], in_=ones[:, 0:1], func=ACT.Sin)
-        digits = const.tile([P, 16], F32, name="digits")
-        nc.vector.memset(digits[:], 1.0)
-        l_int = const.tile([P, N_LT], I32, name="l_int")
-        nc.gpsimd.iota(l_int[:], pattern=[[P, N_LT]], base=0, channel_multiplier=1)
-        row_int = const.tile([P, P], I32, name="row_int")
-        nc.gpsimd.iota(row_int[:], pattern=[[1, P]], base=TURNED * P, channel_multiplier=0)
+        nc.scalar.activation(out=warm[:], in_=ones[:], func=ACT.Sin)
+        l_col = const.tile([P, N_LT], F32, name="l_col")
+        nc.gpsimd.iota(l_col[:], pattern=[[P, N_LT]], base=0, channel_multiplier=1, allow_small_or_imprecise_dtypes=True)
+        l_neg = const.tile([P, N_LT], F32, name="l_neg")
+        nc.gpsimd.iota(l_neg[:], pattern=[[-P, N_LT]], base=0, channel_multiplier=-1, allow_small_or_imprecise_dtypes=True)
+        l_row = const.tile([P, P], F32, name="l_row")
+        nc.gpsimd.iota(
+            l_row[:], pattern=[[1, P]], base=TURNED * P, channel_multiplier=0, allow_small_or_imprecise_dtypes=True
+        )
         ident32 = const.tile([P, P], F32, name="ident32")
         make_identity(nc, ident32[:])
 
         ctx.enter_context(tc.manual_schedule())
 
-        l_col = const.tile([P, N_LT], F32, name="l_col")
-        nc.vector.tensor_copy(out=l_col[:], in_=l_int[:])
-        for level in range(4):
-            for n in range(4):
-                value = RATIO ** (n * 4**level)
-                if level == 0:
-                    value = value / TWO_PI
-                elif n == 0:
-                    continue
-                c = 4 * level + n
-                nc.vector.tensor_scalar(
-                    out=digits[:, c : c + 1], in0=ones[:, 0:1],
-                    scalar1=value, scalar2=None, op0=ALU.mult,
-                )
-        low = const.tile([P, 16], F32, name="low")
-        high = const.tile([P, 16], F32, name="high")
-        for dst, base in ((low, 0), (high, 8)):
-            nc.vector.tensor_tensor(
-                out=dst[:].rearrange("p (m n) -> p m n", n=4),
-                in0=digits[:, base + 4 : base + 8].unsqueeze(2).to_broadcast([P, 4, 4]),
-                in1=digits[:, base : base + 4].unsqueeze(1).to_broadcast([P, 4, 4]),
-                op=ALU.mult,
-            )
         turns = const.tile([P, HALF], F32, name="turns")
-        nc.vector.tensor_tensor(
-            out=turns[:].rearrange("p (m n) -> p m n", n=16),
-            in0=high[:].unsqueeze(2).to_broadcast([P, 16, 16]),
-            in1=low[:].unsqueeze(1).to_broadcast([P, 16, 16]),
-            op=ALU.mult,
-        )
+        for n in range(4):
+            nc.vector.tensor_scalar(
+                out=turns[:, n : n + 1], in0=ones[:], scalar1=RATIO**n / TWO_PI, scalar2=None, op0=ALU.mult
+            )
+        for level in range(1, 4):
+            size = 4**level
+            for n in range(1, 4):
+                nc.vector.tensor_scalar(
+                    out=turns[:, n * size : (n + 1) * size], in0=turns[:, 0:size],
+                    scalar1=RATIO ** (n * size), scalar2=None, op0=ALU.mult,
+                )
 
         omega = const.tile([P, HALF], F32, name="omega")
-        nc.vector.tensor_scalar(out=omega[:], in0=turns[:], scalar1=TWO_PI, scalar2=None, op0=ALU.mult)
-        l_neg = const.tile([P, N_LT], F32, name="l_neg")
-        nc.vector.tensor_scalar(out=l_neg[:], in0=l_col[:], scalar1=-1.0, scalar2=None, op0=ALU.mult)
+        nc.scalar.activation(out=omega[:], in_=turns[:], func=ACT.Copy, scale=TWO_PI)
 
         whole = {}
         frac = {}
@@ -123,11 +105,11 @@ def tile_retention_pa_kernel(tc, X_bytes, X_scale, W_Q, W_K, out_0, out_1):
 
         def table_whole(a):
             cut = first_direct(a)
-            wh = const.tile([P, 3, cut], U32, name="whole%d" % a)
+            wh = const.tile([P, 3, cut], I32, name="whole%d" % a)
             for j, phi in enumerate(PHASES):
-                nc.scalar.activation(
-                    out=wh[:, j, :], in_=turns[:, 0:cut], func=ACT.Copy,
-                    scale=l_col[:, a : a + 1], bias=phi,
+                nc.vector.tensor_scalar(
+                    out=wh[:, j, :], in0=turns[:, 0:cut], scalar1=l_col[:, a : a + 1], scalar2=phi,
+                    op0=ALU.mult, op1=ALU.add,
                 )
             whole[a] = wh
 
@@ -136,7 +118,7 @@ def tile_retention_pa_kernel(tc, X_bytes, X_scale, W_Q, W_K, out_0, out_1):
             fr = const.tile([P, 3, cut], F32, name="frac%d" % a)
             nc.vector.scalar_tensor_tensor(
                 out=fr[:], in0=turns[:, 0:cut].unsqueeze(1).to_broadcast([P, 3, cut]),
-                scalar=l_col[:, a : a + 1], in1=whole[a][:].bitcast(I32),
+                scalar=l_col[:, a : a + 1], in1=whole[a][:],
                 op0=ALU.mult, op1=ALU.subtract,
             )
             frac[a] = fr
@@ -162,26 +144,21 @@ def tile_retention_pa_kernel(tc, X_bytes, X_scale, W_Q, W_K, out_0, out_1):
                 nc.tensor.transpose(vt[:, tau, :], turns[:, tau * P : (tau + 1) * P], ident32[:])
             turned_consts["vt"] = vt
 
-        def turned_prepare_vector():
-            v_col = const.tile([P, 2], F32, name="v_col")
-            nc.vector.tensor_copy(out=v_col[:], in_=turned_consts["vt"][:, :, 0])
-            w_col = const.tile([P, 2], F32, name="w_col")
-            nc.vector.tensor_scalar(out=w_col[:], in0=v_col[:], scalar1=TWO_PI, scalar2=None, op0=ALU.mult)
-            w_neg = const.tile([P, 2], F32, name="w_neg")
-            nc.vector.tensor_scalar(out=w_neg[:], in0=v_col[:], scalar1=-TWO_PI, scalar2=None, op0=ALU.mult)
-            l_row = const.tile([P, P], F32, name="l_row")
-            nc.vector.tensor_copy(out=l_row[:], in_=row_int[:])
-            turned_consts["v_col"] = v_col
-            turned_consts["w_col"] = w_col
-            turned_consts["w_neg"] = w_neg
+        def turned_prepare_scalar():
+            for key, factor in (("v_col", 1.0), ("w_col", TWO_PI), ("w_neg", -TWO_PI)):
+                column = const.tile([P, 2], F32, name=key)
+                nc.scalar.activation(
+                    out=column[:], in_=turned_consts["vt"][:, :, 0], func=ACT.Copy, scale=factor,
+                )
+                turned_consts[key] = column
             turned_consts["l_row"] = l_row
 
         def turned_whole():
-            wh = const.tile([P, 3, P], U32, name="whole_t")
+            wh = const.tile([P, 3, P], I32, name="whole_t")
             for j, phi in enumerate(PHASES):
-                nc.scalar.activation(
-                    out=wh[:, j, :], in_=turned_consts["l_row"][:], func=ACT.Copy,
-                    scale=turned_consts["v_col"][:, 0:1], bias=phi,
+                nc.vector.tensor_scalar(
+                    out=wh[:, j, :], in0=turned_consts["l_row"][:], scalar1=turned_consts["v_col"][:, 0:1],
+                    scalar2=phi, op0=ALU.mult, op1=ALU.add,
                 )
             turned_consts["whole"] = wh
 
@@ -189,7 +166,7 @@ def tile_retention_pa_kernel(tc, X_bytes, X_scale, W_Q, W_K, out_0, out_1):
             fr = const.tile([P, 3, P], F32, name="frac_t")
             nc.vector.scalar_tensor_tensor(
                 out=fr[:], in0=turned_consts["l_row"][:].unsqueeze(1).to_broadcast([P, 3, P]),
-                scalar=turned_consts["v_col"][:, 0:1], in1=turned_consts["whole"][:].bitcast(I32),
+                scalar=turned_consts["v_col"][:, 0:1], in1=turned_consts["whole"][:],
                 op0=ALU.mult, op1=ALU.subtract,
             )
             turned_consts["frac"] = fr
@@ -442,13 +419,17 @@ def tile_retention_pa_kernel(tc, X_bytes, X_scale, W_Q, W_K, out_0, out_1):
         turned_prepare_tensor()
         table_whole(0)
         table_frac(0)
-        turned_prepare_vector()
+        table_whole(1)
+        table_frac(1)
         x_cast(0)
         x_turn(0)
+        turned_prepare_scalar()
         x_cast(1)
         x_scale(0)
         weight_copy(0)
         weight_quant(0)
+        table_whole(3)
+        table_frac(3)
         x_weave(0)
         weight_copy(1)
         x_quant(0)
@@ -458,12 +439,12 @@ def tile_retention_pa_kernel(tc, X_bytes, X_scale, W_Q, W_K, out_0, out_1):
         x_scale(1)
         x_weave(1)
         x_cast(2)
-        table_whole(1)
         mx(0)
-        fractions = {0: lambda: table_frac(1), 4: turned_frac, 6: lambda: table_frac(3)}
+        turned_whole()
+        turned_frac()
+        fractions = {}
         scalar_tables = {
-            1: (lambda: table_sin(1),), 3: (turned_whole,), 5: (turned_sin, lambda: table_whole(3)),
-            7: (lambda: table_sin(3),),
+            1: (lambda: table_sin(1),), 5: (turned_sin,), 7: (lambda: table_sin(3),),
         }
         waiting = []
         for r in range(N_ROWS):

@@ -29,8 +29,14 @@ RATIO = 10000.0 ** (-1.0 / 255.0)
 PHASES = (-0.125, 0.625, 0.25)
 DIRECT_BIAS = (-0.25 * math.pi, -0.75 * math.pi, 0.5 * math.pi)
 V_HALVES = ()
+WHOLE = (10, 11, 12, 13)
 G_WEAVES = (0,)
-PAIRS = ((0, 0), (0, 1), (1, 0), (1, 1), (2, 0), (3, 0), (3, 1), (2, 1))
+ROWS = (
+    (0, 0), (0, 1), (0, 2), (0, 3), (1, 0), (1, 1), (1, 2), (1, 3),
+    (2, 0), (2, 1), (3, 0), (3, 1), (3, 2), (3, 3), (2, 2), (2, 3),
+)
+SINES = {1: 1, 5: 2, 7: 3}
+LOADS = (1, 2, 3)
 TURNED = 2
 
 
@@ -63,7 +69,7 @@ def tile_retention_pa_kernel(tc, X_bytes, X_scale, W_Q, W_K, out_0, out_1):
             wr = const.tile([P, 4, D], BF16, name="w_raw%d" % n)
             nc.sync.dma_start(out=wr[:], in_=w.rearrange("(p j) n -> p j n", j=4))
             w_raw.append(wr)
-        for a in range(1, N_LT):
+        for a in LOADS:
             nc.sync.dma_start(out=x_bytes[a][:], in_=x_view[a])
 
         ones = const.tile([P, 1], F32, name="ones")
@@ -190,14 +196,13 @@ def tile_retention_pa_kernel(tc, X_bytes, X_scale, W_Q, W_K, out_0, out_1):
         w_codes = {}
         w_scales = {}
 
-        def weight_copy(n):
-            wg = const.tile([P, 4 * D], BF16, name="w_grouped%d" % n, align_bytes=64)
-            for h in range(2):
-                nc.vector.tensor_copy(
-                    out=wg[:, h * 1024 : (h + 1) * 1024].rearrange("p (i t) -> p i t", t=4),
-                    in_=w_raw[n][:].rearrange("p t (i e) -> p e i t", e=2)[:, 1 - h],
-                )
-            w_grouped[n] = wg
+        def weight_copy(n, h, copy):
+            if h == 0:
+                w_grouped[n] = const.tile([P, 4 * D], BF16, name="w_grouped", tag="w_grouped%d" % n, align_bytes=64)
+            copy(
+                out=w_grouped[n][:, h * 1024 : (h + 1) * 1024].rearrange("p (i t) -> p i t", t=4),
+                in_=w_raw[n][:].rearrange("p t (i e) -> p e i t", e=2)[:, 1 - h],
+            )
 
         def weight_quant(n):
             wc = const.tile([P, D], U32, name="w_codes%d" % n, align_bytes=64)
@@ -212,12 +217,13 @@ def tile_retention_pa_kernel(tc, X_bytes, X_scale, W_Q, W_K, out_0, out_1):
         x_codes = {}
 
         def x_cast(j):
-            a, first = PAIRS[j][0], 2 * PAIRS[j][1]
+            (a, b), (a1, b1) = ROWS[2 * j], ROWS[2 * j + 1]
             wd = work.tile([P, 2 * D], BF16, name="wide", tag="wide")
-            nc.scalar.copy(
-                out=wd[:],
-                in_=x_bytes[a][:, first : first + 2, :].rearrange("p b k -> p (b k)").bitcast(FP8),
-            )
+            if (a1, b1) == (a, b + 1):
+                nc.scalar.copy(out=wd[:], in_=x_bytes[a][:, b : b + 2, :].rearrange("p b k -> p (b k)").bitcast(FP8))
+            else:
+                nc.scalar.copy(out=wd[:, 0:D], in_=x_bytes[a][:, b, :].bitcast(FP8))
+                nc.scalar.copy(out=wd[:, D : 2 * D], in_=x_bytes[a1][:, b1, :].bitcast(FP8))
             wide[j] = wd
 
         def x_turn(j):
@@ -290,7 +296,7 @@ def tile_retention_pa_kernel(tc, X_bytes, X_scale, W_Q, W_K, out_0, out_1):
             banks[r] = got
 
         def mul(r):
-            tp = tables[PAIRS[r // 2][0]]
+            tp = tables[ROWS[r][0]]
             cross = work.tile([P, 2 * D], F32, name="cross", tag="cross", bufs=6)
             common = work.tile([P, D], F32, name="common", tag="common", bufs=6)
             pair = tp[:, 0:2, :].rearrange("p e i -> p i e")
@@ -324,8 +330,8 @@ def tile_retention_pa_kernel(tc, X_bytes, X_scale, W_Q, W_K, out_0, out_1):
             results[r] = res
 
         def store(r, n, queue):
-            a, half = PAIRS[r // 2]
-            queue.dma_start(out=o_views[n][a, 2 * half + r % 2], in_=results[r][:, n * D : (n + 1) * D])
+            a, b = ROWS[r]
+            queue.dma_start(out=o_views[n][a, b], in_=results[r][:, n * D : (n + 1) * D])
 
         def add_on(engine, r, first, count):
             cross, common = parts[r]
@@ -414,7 +420,7 @@ def tile_retention_pa_kernel(tc, X_bytes, X_scale, W_Q, W_K, out_0, out_1):
             store(r, n, nc.scalar)
 
         def is_turned(r):
-            return PAIRS[r // 2][0] == TURNED
+            return ROWS[r][0] == TURNED
 
         turned_prepare_tensor()
         table_whole(0)
@@ -426,12 +432,14 @@ def tile_retention_pa_kernel(tc, X_bytes, X_scale, W_Q, W_K, out_0, out_1):
         turned_prepare_scalar()
         x_cast(1)
         x_scale(0)
-        weight_copy(0)
+        weight_copy(0, 0, nc.vector.tensor_copy)
+        weight_copy(0, 1, nc.vector.tensor_copy)
         weight_quant(0)
         table_whole(3)
         table_frac(3)
         x_weave(0)
-        weight_copy(1)
+        weight_copy(1, 0, nc.scalar.copy)
+        weight_copy(1, 1, nc.vector.tensor_copy)
         x_quant(0)
         weight_quant(1)
         table_sin(0)
@@ -442,10 +450,6 @@ def tile_retention_pa_kernel(tc, X_bytes, X_scale, W_Q, W_K, out_0, out_1):
         mx(0)
         turned_whole()
         turned_frac()
-        fractions = {}
-        scalar_tables = {
-            1: (lambda: table_sin(1),), 5: (turned_sin,), 7: (lambda: table_sin(3),),
-        }
         waiting = []
         for r in range(N_ROWS):
             j = r // 2
@@ -476,10 +480,8 @@ def tile_retention_pa_kernel(tc, X_bytes, X_scale, W_Q, W_K, out_0, out_1):
             if r % 2 == 0:
                 if j + 1 < N_PAIRS:
                     x_quant(j + 1)
-            if r in fractions:
-                fractions[r]()
             by_vector = [n for n in range(2) if (r, n) in V_HALVES]
-            if not is_turned(r) and PAIRS[j][0] == 3:
+            if not is_turned(r) and r in WHOLE:
                 add_on(nc.gpsimd, r, 0, 2)
                 for n in range(2):
                     store(r, n, nc.sync)
@@ -494,8 +496,10 @@ def tile_retention_pa_kernel(tc, X_bytes, X_scale, W_Q, W_K, out_0, out_1):
                 if j + 2 < N_PAIRS:
                     x_scale(j + 2)
                     x_weave(j + 2)
-            for step in scalar_tables.get(r, ()):
-                step()
+            if SINES.get(r) == TURNED:
+                turned_sin()
+            elif r in SINES:
+                table_sin(SINES[r])
             for unit in now:
                 turn_add_out(unit[0], unit[1])
             for n in by_vector:

import math
from contextlib import ExitStack

import concourse.mybir as mybir
from concourse.masks import make_identity

FLOPS = 2 * 2 * 2048 * 512 * 512

F32 = mybir.dt.float32
BF16 = mybir.dt.bfloat16
I32 = mybir.dt.int32
U32 = mybir.dt.uint32
U8 = mybir.dt.uint8
FP8 = mybir.dt.float8_e4m3fn
FP8X4 = mybir.dt.float8_e4m3fn_x4
ALU = mybir.AluOpType
ACT = mybir.ActivationFunctionType

P = 128
D = 512
HALF = 256
N_LT = 4
N_BH = 4
N_ROWS = 16
N_PAIRS = 8
TWO_PI = 2.0 * math.pi
ROOT2 = math.sqrt(2.0)
RATIO = 10000.0 ** (-1.0 / 255.0)
PHASES = (-0.125, 0.625, 0.25)
DIRECT_BIAS = (-0.25 * math.pi, -0.75 * math.pi, 0.5 * math.pi)
V_HALVES = ()
WHOLE = (10, 11, 12, 13)
G_WEAVES = (0,)
ROWS = (
    (0, 0), (0, 1), (0, 2), (0, 3), (1, 0), (1, 1), (1, 2), (1, 3),
    (2, 0), (2, 1), (3, 0), (3, 1), (3, 2), (3, 3), (2, 2), (2, 3),
)
SINES = {1: 1, 5: 2, 7: 3}
LOADS = (1, 2, 3)
TURNED = 2


def first_direct(a):
    return min([i for i in range(0, HALF, 8) if (P * a + P - 1) * RATIO**i <= 1.2 * math.pi])


def tile_retention_pa_kernel(tc, X_bytes, X_scale, W_Q, W_K, out_0, out_1):
    nc = tc.nc
    x_view = X_bytes.rearrange("b h (a p) k -> a p (b h) k", p=P)
    o_views = (
        out_0.rearrange("b h (a p) d -> a (b h) p d", p=P),
        out_1.rearrange("b h (a p) d -> a (b h) p d", p=P),
    )

    with ExitStack() as ctx:
        const = ctx.enter_context(tc.tile_pool(name="const", bufs=1))
        work = ctx.enter_context(tc.tile_pool(name="work", bufs=3))
        psum = ctx.enter_context(tc.psum_pool(name="psum", bufs=2))

        x_bytes = []
        for a in range(N_LT):
            xb = const.tile([P, N_BH, D], U8, name="x_bytes%d" % a)
            x_bytes.append(xb)
        nc.sync.dma_start(out=x_bytes[0][:], in_=x_view[0])
        scale_pt = const.tile([P, 4], F32, name="scale_pt")
        nc.sync.dma_start(out=scale_pt[:], in_=X_scale.rearrange("a b c (p t) -> p (a b c t)", t=4))
        w_raw = []
        for n, w in enumerate((W_Q, W_K)):
            wr = const.tile([P, 4, D], BF16, name="w_raw%d" % n)
            nc.sync.dma_start(out=wr[:], in_=w.rearrange("(p j) n -> p j n", j=4))
            w_raw.append(wr)
        for a in LOADS:
            nc.sync.dma_start(out=x_bytes[a][:], in_=x_view[a])

        ones = const.tile([P, 1], F32, name="ones")
        nc.vector.memset(ones[:], 1.0)
        warm = const.tile([P, 1], F32, name="warm")
        nc.scalar.activation(out=warm[:], in_=ones[:], func=ACT.Sin)
        l_col = const.tile([P, N_LT], F32, name="l_col")
        nc.gpsimd.iota(l_col[:], pattern=[[P, N_LT]], base=0, channel_multiplier=1, allow_small_or_imprecise_dtypes=True)
        l_neg = const.tile([P, N_LT], F32, name="l_neg")
        nc.gpsimd.iota(l_neg[:], pattern=[[-P, N_LT]], base=0, channel_multiplier=-1, allow_small_or_imprecise_dtypes=True)
        l_row = const.tile([P, P], F32, name="l_row")
        nc.gpsimd.iota(
            l_row[:], pattern=[[1, P]], base=TURNED * P, channel_multiplier=0, allow_small_or_imprecise_dtypes=True
        )
        ident32 = const.tile([P, P], F32, name="ident32")
        make_identity(nc, ident32[:])

        ctx.enter_context(tc.manual_schedule())

        turns = const.tile([P, HALF], F32, name="turns")
        for n in range(4):
            nc.vector.tensor_scalar(
                out=turns[:, n : n + 1], in0=ones[:], scalar1=RATIO**n / TWO_PI, scalar2=None, op0=ALU.mult
            )
        for level in range(1, 4):
            size = 4**level
            for n in range(1, 4):
                nc.vector.tensor_scalar(
                    out=turns[:, n * size : (n + 1) * size], in0=turns[:, 0:size],
                    scalar1=RATIO ** (n * size), scalar2=None, op0=ALU.mult,
                )

        omega = const.tile([P, HALF], F32, name="omega")
        nc.scalar.activation(out=omega[:], in_=turns[:], func=ACT.Copy, scale=TWO_PI)

        whole = {}
        frac = {}
        tables = {}

        def table_whole(a):
            cut = first_direct(a)
            wh = const.tile([P, 3, cut], I32, name="whole%d" % a)
            for j, phi in enumerate(PHASES):
                nc.vector.tensor_scalar(
                    out=wh[:, j, :], in0=turns[:, 0:cut], scalar1=l_col[:, a : a + 1], scalar2=phi,
                    op0=ALU.mult, op1=ALU.add,
                )
            whole[a] = wh

        def table_frac(a):
            cut = first_direct(a)
            fr = const.tile([P, 3, cut], F32, name="frac%d" % a)
            nc.vector.scalar_tensor_tensor(
                out=fr[:], in0=turns[:, 0:cut].unsqueeze(1).to_broadcast([P, 3, cut]),
                scalar=l_col[:, a : a + 1], in1=whole[a][:],
                op0=ALU.mult, op1=ALU.subtract,
            )
            frac[a] = fr

        def table_sin(a):
            tp = const.tile([P, 3, HALF], F32, name="table%d" % a)
            tables[a] = tp
            cut = first_direct(a)
            for j, phi in enumerate(PHASES):
                l_signed = l_neg if j == 2 else l_col
                pieces = (
                    (0, cut, frac[a][:, j, :], TWO_PI, TWO_PI * phi),
                    (cut, HALF, omega[:, cut:HALF], l_signed[:, a : a + 1], DIRECT_BIAS[j]),
                )
                for lo, hi, src, scale, bias in pieces:
                    nc.scalar.activation(out=tp[:, j, lo:hi], in_=src, func=ACT.Sin, scale=scale, bias=bias)

        turned_consts = {}

        def turned_prepare_tensor():
            vt = psum.tile([P, 2, P], F32, name="vt", tag="aux")
            for tau in range(2):
                nc.tensor.transpose(vt[:, tau, :], turns[:, tau * P : (tau + 1) * P], ident32[:])
            turned_consts["vt"] = vt

        def turned_prepare_scalar():
            for key, factor in (("v_col", 1.0), ("w_col", TWO_PI), ("w_neg", -TWO_PI)):
                column = const.tile([P, 2], F32, name=key)
                nc.scalar.activation(
                    out=column[:], in_=turned_consts["vt"][:, :, 0], func=ACT.Copy, scale=factor,
                )
                turned_consts[key] = column
            turned_consts["l_row"] = l_row

        def turned_whole():
            wh = const.tile([P, 3, P], I32, name="whole_t")
            for j, phi in enumerate(PHASES):
                nc.vector.tensor_scalar(
                    out=wh[:, j, :], in0=turned_consts["l_row"][:], scalar1=turned_consts["v_col"][:, 0:1],
                    scalar2=phi, op0=ALU.mult, op1=ALU.add,
                )
            turned_consts["whole"] = wh

        def turned_frac():
            fr = const.tile([P, 3, P], F32, name="frac_t")
            nc.vector.scalar_tensor_tensor(
                out=fr[:], in0=turned_consts["l_row"][:].unsqueeze(1).to_broadcast([P, 3, P]),
                scalar=turned_consts["v_col"][:, 0:1], in1=turned_consts["whole"][:],
                op0=ALU.mult, op1=ALU.subtract,
            )
            turned_consts["frac"] = fr

        def turned_sin():
            assert first_direct(TURNED) <= P
            tp = const.tile([P, 3, 2, P], F32, name="table_t")
            for j, phi in enumerate(PHASES):
                nc.scalar.activation(
                    out=tp[:, j, 0, :], in_=turned_consts["frac"][:, j, :], func=ACT.Sin,
                    scale=TWO_PI, bias=TWO_PI * phi,
                )
                w_signed = turned_consts["w_neg"] if j == 2 else turned_consts["w_col"]
                nc.scalar.activation(
                    out=tp[:, j, 1, :], in_=turned_consts["l_row"][:], func=ACT.Sin,
                    scale=w_signed[:, 1:2], bias=DIRECT_BIAS[j],
                )
            turned_consts["table"] = tp

        w_grouped = {}
        w_codes = {}
        w_scales = {}

        def weight_copy(n, h, copy):
            if h == 0:
                w_grouped[n] = const.tile([P, 4 * D], BF16, name="w_grouped", tag="w_grouped%d" % n, align_bytes=64)
            copy(
                out=w_grouped[n][:, h * 1024 : (h + 1) * 1024].rearrange("p (i t) -> p i t", t=4),
                in_=w_raw[n][:].rearrange("p t (i e) -> p e i t", e=2)[:, 1 - h],
            )

        def weight_quant(n):
            wc = const.tile([P, D], U32, name="w_codes%d" % n, align_bytes=64)
            ws = const.tile([P, D], U8, name="w_scales%d" % n, align_bytes=64)
            nc.vector.quantize_mx(out=wc[:].bitcast(FP8X4), scales=ws[:], in_=w_grouped[n][:])
            w_codes[n] = wc
            w_scales[n] = ws

        wide = {}
        turned = {}
        grouped = {}
        x_codes = {}

        def x_cast(j):
            (a, b), (a1, b1) = ROWS[2 * j], ROWS[2 * j + 1]
            wd = work.tile([P, 2 * D], BF16, name="wide", tag="wide")
            if (a1, b1) == (a, b + 1):
                nc.scalar.copy(out=wd[:], in_=x_bytes[a][:, b : b + 2, :].rearrange("p b k -> p (b k)").bitcast(FP8))
            else:
                nc.scalar.copy(out=wd[:, 0:D], in_=x_bytes[a][:, b, :].bitcast(FP8))
                nc.scalar.copy(out=wd[:, D : 2 * D], in_=x_bytes[a1][:, b1, :].bitcast(FP8))
            wide[j] = wd

        def x_turn(j):
            xt = psum.tile([P, 2, 2, P], F32, name="xt", tag="aux")
            words = wide[j][:].bitcast(F32)
            for s in range(2):
                for u in range(2):
                    nc.tensor.transpose(xt[:, u, s, :], words[:, s * HALF + u : (s + 1) * HALF : 2], ident32[:])
            turned[j] = xt

        def x_scale(j):
            planes = work.tile([P, 4, 2 * P], BF16, name="planes", tag="planes", bufs=2)
            for t in range(4):
                nc.scalar.activation(
                    out=planes[:, t, :],
                    in_=turned[j][:, t // 2].rearrange("p s r -> p (s r)").bitcast(BF16)
                    .rearrange("p (c e) -> p c e", e=2)[:, :, t % 2],
                    func=ACT.Copy, scale=scale_pt[:, t : t + 1],
                )
            turned[j] = planes

        def x_weave(j):
            gr = work.tile([P, 1024], BF16, name="grouped", tag="grouped", align_bytes=64)
            if j in G_WEAVES:
                nc.vector.tensor_copy(
                    out=gr[:].rearrange("p (c t) -> p c t", t=4),
                    in_=turned[j][:].rearrange("p t c -> p c t"),
                )
            else:
                nc.scalar.copy(
                    out=gr[:].rearrange("p (c i t) -> p c t i", i=4, t=4),
                    in_=turned[j][:].rearrange("p t (c i) -> p c t i", i=4),
                )
            grouped[j] = gr

        def x_quant(j):
            xc = work.tile([P, HALF], U32, name="xc", tag="xc", align_bytes=64)
            xsc = work.tile([P, HALF], U8, name="xsc", tag="xsc", align_bytes=64)
            nc.vector.quantize_mx(out=xc[:].bitcast(FP8X4), scales=xsc[:], in_=grouped[j][:])
            x_codes[j] = (xc, xsc)

        banks = {}
        parts = {}
        results = {}

        def mx(r):
            xc, xsc = x_codes[r // 2]
            rows = slice((r % 2) * P, (r % 2 + 1) * P)
            lhs = xc[:, rows].bitcast(FP8X4)
            lhs_s = xsc[:, rows]
            got = []
            for n in range(2):
                acc = psum.tile([P, D], F32, name="acc%d" % n, tag="acc%d" % n)
                nc.tensor.matmul_mx(
                    out=acc[:], lhsT=lhs, lhsT_scale=lhs_s,
                    rhs=w_codes[n][:].bitcast(FP8X4), rhs_scale=w_scales[n][:],
                    start=True, stop=True,
                )
                got.append(acc)
            sums = psum.tile([P, D], F32, name="sums", tag="sums")
            for n in range(2):
                for h in range(2):
                    cols = slice(h * HALF, (h + 1) * HALF)
                    nc.tensor.matmul_mx(
                        out=sums[:, n * HALF : (n + 1) * HALF], lhsT=lhs, lhsT_scale=lhs_s,
                        rhs=w_codes[n][:, cols].bitcast(FP8X4), rhs_scale=w_scales[n][:, cols],
                        start=(h == 0), stop=(h == 1),
                    )
            got.append(sums)
            banks[r] = got

        def mul(r):
            tp = tables[ROWS[r][0]]
            cross = work.tile([P, 2 * D], F32, name="cross", tag="cross", bufs=6)
            common = work.tile([P, D], F32, name="common", tag="common", bufs=6)
            pair = tp[:, 0:2, :].rearrange("p e i -> p i e")

            def side_terms():
                for n in range(2):
                    nc.vector.scalar_tensor_tensor(
                        out=cross[:, n * D : (n + 1) * D].rearrange("p (i e) -> p i e", e=2),
                        in0=banks[r][n][:].rearrange("p (e i) -> p i e", e=2),
                        scalar=ROOT2,
                        in1=pair if n == 1 else pair[:, :, ::-1],
                        op0=ALU.mult, op1=ALU.mult,
                    )

            def shared_term():
                nc.vector.tensor_tensor(
                    out=common[:].rearrange("p (n i) -> p n i", n=2),
                    in0=banks[r][2][:].rearrange("p (n i) -> p n i", n=2),
                    in1=tp[:, 2:3, :].to_broadcast([P, 2, HALF]),
                    op=ALU.mult,
                )

            if r == N_ROWS - 1:
                shared_term()
                side_terms()
            else:
                side_terms()
                shared_term()
            parts[r] = (cross, common)
            res = work.tile([P, 2 * D], F32, name="res", tag="res", bufs=7)
            results[r] = res

        def store(r, n, queue):
            a, b = ROWS[r]
            queue.dma_start(out=o_views[n][a, b], in_=results[r][:, n * D : (n + 1) * D])

        def add_on(engine, r, first, count):
            cross, common = parts[r]
            nc_cols = slice(first * D, (first + count) * D)
            engine.tensor_tensor(
                out=results[r][:, nc_cols].rearrange("p (m e) -> p m e", e=2),
                in0=common[:, first * HALF : (first + count) * HALF].unsqueeze(2).to_broadcast([P, count * HALF, 2]),
                in1=cross[:, nc_cols].rearrange("p (m e) -> p m e", e=2),
                op=ALU.add,
            )

        def mx_turned(r):
            xc, xsc = x_codes[r // 2]
            rows = slice((r % 2) * P, (r % 2 + 1) * P)
            rhs = xc[:, rows].bitcast(FP8X4)
            rhs_s = xsc[:, rows]
            sums = psum.tile([P, D], F32, name="sums", tag="sums")
            for n in range(2):
                for tau in range(2):
                    for h in range(2):
                        cols = slice((2 * h + tau) * P, (2 * h + tau + 1) * P)
                        nc.tensor.matmul_mx(
                            out=sums[:, (2 * n + tau) * P : (2 * n + tau + 1) * P],
                            lhsT=w_codes[n][:, cols].bitcast(FP8X4), lhsT_scale=w_scales[n][:, cols],
                            rhs=rhs, rhs_scale=rhs_s, start=(h == 0), stop=(h == 1),
                        )
            got = []
            for n in range(2):
                acc = psum.tile([P, D], F32, name="acc%d" % n, tag="acc%d" % n)
                for blk in range(4):
                    cols = slice(blk * P, (blk + 1) * P)
                    nc.tensor.matmul_mx(
                        out=acc[:, cols], lhsT=w_codes[n][:, cols].bitcast(FP8X4), lhsT_scale=w_scales[n][:, cols],
                        rhs=rhs, rhs_scale=rhs_s, start=True, stop=True,
                    )
                got.append(acc)
            got.append(sums)
            banks[r] = got

        def mul_turned(r):
            tp = turned_consts["table"]
            cross = work.tile([P, 2 * D], F32, name="cross", tag="cross", bufs=6)
            common = work.tile([P, D], F32, name="common", tag="common", bufs=6)
            nc.vector.tensor_tensor(
                out=common[:].rearrange("p (n m) -> p n m", n=2),
                in0=banks[r][2][:].rearrange("p (n m) -> p n m", n=2),
                in1=tp[:, 2:3].rearrange("p e t l -> p e (t l)").to_broadcast([P, 2, HALF]),
                op=ALU.mult,
            )
            pair = tp[:, 0:2].rearrange("p e t l -> p e (t l)")
            for n in range(2):
                nc.vector.scalar_tensor_tensor(
                    out=cross[:, n * D : (n + 1) * D].rearrange("p (e m) -> p e m", e=2),
                    in0=banks[r][n][:].rearrange("p (e m) -> p e m", e=2),
                    scalar=ROOT2,
                    in1=pair if n == 1 else pair[:, ::-1, :],
                    op0=ALU.mult, op1=ALU.mult,
                )
            parts[r] = (cross, common)
            res = work.tile([P, 2 * D], F32, name="res", tag="res", bufs=7)
            results[r] = res

        added = {}

        def turn_add(r, n):
            cross, common = parts[r]
            total = psum.tile([P, D], F32, name="total", tag="aux")
            for e in range(2):
                for tau in range(2):
                    region = total[:, (2 * e + tau) * P : (2 * e + tau + 1) * P]
                    nc.tensor.matmul(
                        out=region, lhsT=common[:, (2 * n + tau) * P : (2 * n + tau + 1) * P], rhs=ident32[:],
                        is_transpose=True, start=True, stop=False,
                    )
                    nc.tensor.matmul(
                        out=region, lhsT=cross[:, n * D + (2 * e + tau) * P : n * D + (2 * e + tau + 1) * P],
                        rhs=ident32[:], is_transpose=True, start=False, stop=True,
                    )
            added[(r, n)] = total

        def turn_add_out(r, n):
            nc.scalar.copy(
                out=results[r][:, n * D : (n + 1) * D].rearrange("p (m e) -> p m e", e=2),
                in_=added[(r, n)][:].rearrange("p (e m) -> p m e", e=2),
            )
            store(r, n, nc.scalar)

        def is_turned(r):
            return ROWS[r][0] == TURNED

        turned_prepare_tensor()
        table_whole(0)
        table_frac(0)
        table_whole(1)
        table_frac(1)
        x_cast(0)
        x_turn(0)
        turned_prepare_scalar()
        x_cast(1)
        x_scale(0)
        weight_copy(0, 0, nc.vector.tensor_copy)
        weight_copy(0, 1, nc.vector.tensor_copy)
        weight_quant(0)
        table_whole(3)
        table_frac(3)
        x_weave(0)
        weight_copy(1, 0, nc.scalar.copy)
        weight_copy(1, 1, nc.vector.tensor_copy)
        x_quant(0)
        weight_quant(1)
        table_sin(0)
        x_turn(1)
        x_scale(1)
        x_weave(1)
        x_cast(2)
        mx(0)
        turned_whole()
        turned_frac()
        waiting = []
        for r in range(N_ROWS):
            j = r // 2
            if r % 2 == 0:
                if j + 2 < N_PAIRS:
                    x_turn(j + 2)
                if j + 3 < N_PAIRS:
                    x_cast(j + 3)
            if r + 1 < N_ROWS:
                if is_turned(r + 1):
                    mx_turned(r + 1)
                else:
                    mx(r + 1)
            now = waiting[0:1]
            for unit in now:
                waiting.remove(unit)
                turn_add(unit[0], unit[1])
            if is_turned(r):
                mul_turned(r)
                waiting.extend([(r, 0), (r, 1)])
            else:
                mul(r)
            if r >= N_ROWS - 2:
                for unit in waiting:
                    turn_add(unit[0], unit[1])
                now = now + waiting
                waiting = []
            if r % 2 == 0:
                if j + 1 < N_PAIRS:
                    x_quant(j + 1)
            by_vector = [n for n in range(2) if (r, n) in V_HALVES]
            if not is_turned(r) and r in WHOLE:
                add_on(nc.gpsimd, r, 0, 2)
                for n in range(2):
                    store(r, n, nc.sync)
            elif not is_turned(r):
                for n in range(2):
                    if n in by_vector:
                        add_on(nc.vector, r, n, 1)
                    else:
                        add_on(nc.gpsimd, r, n, 1)
                        store(r, n, nc.sync)
            if r % 2 == 0:
                if j + 2 < N_PAIRS:
                    x_scale(j + 2)
                    x_weave(j + 2)
            if SINES.get(r) == TURNED:
                turned_sin()
            elif r in SINES:
                table_sin(SINES[r])
            for unit in now:
                turn_add_out(unit[0], unit[1])
            for n in by_vector:
                store(r, n, nc.scalar)
